import numpy as np
import ml_dtypes

BF16 = ml_dtypes.bfloat16


def bf(x):
    return np.asarray(x, np.float32).astype(BF16)


def f32(x):
    return np.asarray(x, np.float32)


def f64(x):
    return np.asarray(x).astype(np.float64)


def striped(idx):
    return np.tile(idx.reshape(-1, 16).T, (8, 1))


D, S, N = 128, 512, 256


def view(h, item, w_out, b_out):
    return np.maximum(f64(w_out).T @ (f64(h) + f64(item)) + f64(b_out), 0.0)


def setup_inputs():
    return {
        "base": f32(np.random.standard_normal((D, S))),
        "h0": f32(np.random.standard_normal((D, N))),
        "item0": f32(np.random.standard_normal((D, N))),
        "h1": f32(np.random.standard_normal((D, N))),
        "item1": f32(np.random.standard_normal((D, N))),
        "w_out": bf(np.random.standard_normal((D, D)) / np.sqrt(D)),
        "b_out": f32(0.3 * np.random.standard_normal((D, 1))),
        "offs": striped(np.random.permutation(S)[:N]),
    }


def reference(base, h0, item0, h1, item1, w_out, b_out, offs):
    idx = offs[:16].T.reshape(-1)
    res = f64(base).copy()
    res[:, idx] = 0.5 * view(h0, item0, w_out, b_out) + 0.5 * view(h1, item1, w_out, b_out)
    return res

@@ -1,0 +1,44 @@
+import concourse.mybir as mybir
+
+F32, BF16, U16 = mybir.dt.float32, mybir.dt.bfloat16, mybir.dt.uint16
+ADD = mybir.AluOpType.add
+RELU = mybir.ActivationFunctionType.Relu
+
+D, S, N = 128, 512, 256
+FLOPS = 2 * 2 * D * D * N
+
+
+def tile_kgmodel_kernel(tc, base, h0, item0, h1, item1, w_out, b_out, offs, out):
+    nc = tc.nc
+    with tc.tile_pool(name="held", bufs=1) as held, tc.psum_pool(name="psum", bufs=1) as psum:
+        offsets = held.tile([D, N // 16], U16, name="offsets")
+        nc.sync.dma_start(offsets[:], offs)
+
+        neighbours = [held.tile([D, N], F32, name=f"neighbours{v}") for v in range(2)]
+        items = [held.tile([D, N], F32, name=f"items{v}") for v in range(2)]
+        for v, (h, item) in enumerate(((h0, item0), (h1, item1))):
+            nc.sync.dma_start(neighbours[v][:], h)
+            nc.scalar.dma_start(items[v][:], item)
+
+        weights = held.tile([D, D], BF16, name="weights")
+        nc.gpsimd.dma_start(weights[:], w_out)
+        bias = held.tile([D, 1], F32, name="bias")
+        nc.gpsimd.dma_start(bias[:], b_out)
+        store = held.tile([D, S], F32, name="store")
+        nc.gpsimd.dma_start(store[:], base)
+
+        half_bias = held.tile([D, 1], F32, name="half_bias")
+        nc.vector.tensor_scalar_mul(half_bias[:], bias[:], 0.5)
+
+        half_views = []
+        for v in range(2):
+            summed = held.tile([D, N], BF16, name=f"summed{v}")
+            nc.vector.tensor_tensor(summed[:], neighbours[v][:], items[v][:], ADD)
+            product = psum.tile([D, N], F32, name=f"product{v}")
+            nc.tensor.matmul(product[:], weights[:], summed[:], start=True, stop=True)
+            half_view = held.tile([D, N], F32, name=f"half_view{v}")
+            nc.scalar.activation(half_view[:], product[:], RELU, bias=half_bias[:], scale=0.5)
+            half_views.append(half_view)
+
+        nc.vector.tensor_tensor(store[:].indirect(offsets[:]), half_views[0][:], half_views[1][:], ADD)
+        nc.sync.dma_start(out, store[:])

@@ -11,24 +11,23 @@ FLOPS = 2 * 2 * D * D * N
 def tile_kgmodel_kernel(tc, base, h0, item0, h1, item1, w_out, b_out, offs, out):
     nc = tc.nc
     with tc.tile_pool(name="held", bufs=1) as held, tc.psum_pool(name="psum", bufs=1) as psum:
-        offsets = held.tile([D, N // 16], U16, name="offsets")
-        nc.sync.dma_start(offsets[:], offs)
-
+        weights = held.tile([D, D], BF16, name="weights")
+        nc.sync.dma_start(weights[:], w_out)
+        bias = held.tile([D, 1], F32, name="bias")
+        nc.scalar.dma_start(bias[:], b_out)
         neighbours = [held.tile([D, N], F32, name=f"neighbours{v}") for v in range(2)]
         items = [held.tile([D, N], F32, name=f"items{v}") for v in range(2)]
         for v, (h, item) in enumerate(((h0, item0), (h1, item1))):
             nc.sync.dma_start(neighbours[v][:], h)
             nc.scalar.dma_start(items[v][:], item)
 
-        weights = held.tile([D, D], BF16, name="weights")
-        nc.gpsimd.dma_start(weights[:], w_out)
-        bias = held.tile([D, 1], F32, name="bias")
-        nc.gpsimd.dma_start(bias[:], b_out)
+        offsets = held.tile([D, N // 16], U16, name="offsets")
+        nc.sync.dma_start(offsets[:], offs)
         store = held.tile([D, S], F32, name="store")
         nc.gpsimd.dma_start(store[:], base)
 
         half_bias = held.tile([D, 1], F32, name="half_bias")
-        nc.vector.tensor_scalar_mul(half_bias[:], bias[:], 0.5)
+        nc.scalar.mul(half_bias[:], bias[:], 0.5)
 
         half_views = []
         for v in range(2):

@@ -24,7 +24,7 @@ def tile_kgmodel_kernel(tc, base, h0, item0, h1, item1, w_out, b_out, offs, out)
         offsets = held.tile([D, N // 16], U16, name="offsets")
         nc.sync.dma_start(offsets[:], offs)
         store = held.tile([D, S], F32, name="store")
-        nc.gpsimd.dma_start(store[:], base)
+        nc.scalar.dma_start(store[:], base)
 
         half_bias = held.tile([D, 1], F32, name="half_bias")
         nc.scalar.mul(half_bias[:], bias[:], 0.5)

@@ -10,34 +10,37 @@ FLOPS = 2 * 2 * D * D * N
 
 def tile_kgmodel_kernel(tc, base, h0, item0, h1, item1, w_out, b_out, offs, out):
     nc = tc.nc
+    views = ((h0, item0), (h1, item1))
+    pieces = ((0, 0, N), (1, 0, N // 2), (1, N // 2, N))
+
     with tc.tile_pool(name="held", bufs=1) as held, tc.psum_pool(name="psum", bufs=1) as psum:
         weights = held.tile([D, D], BF16, name="weights")
         nc.sync.dma_start(weights[:], w_out)
         bias = held.tile([D, 1], F32, name="bias")
         nc.scalar.dma_start(bias[:], b_out)
-        neighbours = [held.tile([D, N], F32, name=f"neighbours{v}") for v in range(2)]
-        items = [held.tile([D, N], F32, name=f"items{v}") for v in range(2)]
-        for v, (h, item) in enumerate(((h0, item0), (h1, item1))):
-            nc.sync.dma_start(neighbours[v][:], h)
-            nc.scalar.dma_start(items[v][:], item)
+        neighbours, items = [], []
+        for p, (v, lo, hi) in enumerate(pieces):
+            h, item = views[v]
+            neighbours.append(held.tile([D, hi - lo], F32, name=f"neighbours{p}"))
+            nc.sync.dma_start(neighbours[p][:], h[:, lo:hi])
+            items.append(held.tile([D, hi - lo], F32, name=f"items{p}"))
+            nc.scalar.dma_start(items[p][:], item[:, lo:hi])
 
         offsets = held.tile([D, N // 16], U16, name="offsets")
         nc.sync.dma_start(offsets[:], offs)
         store = held.tile([D, S], F32, name="store")
-        nc.scalar.dma_start(store[:], base)
+        nc.gpsimd.dma_start(store[:], base)
 
         half_bias = held.tile([D, 1], F32, name="half_bias")
         nc.scalar.mul(half_bias[:], bias[:], 0.5)
 
-        half_views = []
-        for v in range(2):
-            summed = held.tile([D, N], BF16, name=f"summed{v}")
-            nc.vector.tensor_tensor(summed[:], neighbours[v][:], items[v][:], ADD)
-            product = psum.tile([D, N], F32, name=f"product{v}")
+        half_views = [held.tile([D, N], F32, name=f"half_view{v}") for v in range(2)]
+        for p, (v, lo, hi) in enumerate(pieces):
+            summed = held.tile([D, hi - lo], BF16, name=f"summed{p}")
+            nc.vector.tensor_tensor(summed[:], neighbours[p][:], items[p][:], ADD)
+            product = psum.tile([D, hi - lo], F32, name=f"product{p}")
             nc.tensor.matmul(product[:], weights[:], summed[:], start=True, stop=True)
-            half_view = held.tile([D, N], F32, name=f"half_view{v}")
-            nc.scalar.activation(half_view[:], product[:], RELU, bias=half_bias[:], scale=0.5)
-            half_views.append(half_view)
+            nc.scalar.activation(half_views[v][:, lo:hi], product[:], RELU, bias=half_bias[:], scale=0.5)
 
         nc.vector.tensor_tensor(store[:].indirect(offsets[:]), half_views[0][:], half_views[1][:], ADD)
         nc.sync.dma_start(out, store[:])

@@ -10,21 +10,16 @@ FLOPS = 2 * 2 * D * D * N
 
 def tile_kgmodel_kernel(tc, base, h0, item0, h1, item1, w_out, b_out, offs, out):
     nc = tc.nc
-    views = ((h0, item0), (h1, item1))
-    pieces = ((0, 0, N), (1, 0, N // 2), (1, N // 2, N))
-
     with tc.tile_pool(name="held", bufs=1) as held, tc.psum_pool(name="psum", bufs=1) as psum:
         weights = held.tile([D, D], BF16, name="weights")
         nc.sync.dma_start(weights[:], w_out)
         bias = held.tile([D, 1], F32, name="bias")
         nc.scalar.dma_start(bias[:], b_out)
-        neighbours, items = [], []
-        for p, (v, lo, hi) in enumerate(pieces):
-            h, item = views[v]
-            neighbours.append(held.tile([D, hi - lo], F32, name=f"neighbours{p}"))
-            nc.sync.dma_start(neighbours[p][:], h[:, lo:hi])
-            items.append(held.tile([D, hi - lo], F32, name=f"items{p}"))
-            nc.scalar.dma_start(items[p][:], item[:, lo:hi])
+        neighbours = [held.tile([D, N], F32, name=f"neighbours{v}") for v in range(2)]
+        items = [held.tile([D, N], F32, name=f"items{v}") for v in range(2)]
+        for v, (h, item) in enumerate(((h0, item0), (h1, item1))):
+            nc.sync.dma_start(neighbours[v][:], h)
+            nc.scalar.dma_start(items[v][:], item)
 
         offsets = held.tile([D, N // 16], U16, name="offsets")
         nc.sync.dma_start(offsets[:], offs)
@@ -34,13 +29,16 @@ def tile_kgmodel_kernel(tc, base, h0, item0, h1, item1, w_out, b_out, offs, out)
         half_bias = held.tile([D, 1], F32, name="half_bias")
         nc.scalar.mul(half_bias[:], bias[:], 0.5)
 
-        half_views = [held.tile([D, N], F32, name=f"half_view{v}") for v in range(2)]
-        for p, (v, lo, hi) in enumerate(pieces):
-            summed = held.tile([D, hi - lo], BF16, name=f"summed{p}")
-            nc.vector.tensor_tensor(summed[:], neighbours[p][:], items[p][:], ADD)
-            product = psum.tile([D, hi - lo], F32, name=f"product{p}")
+        half_views = []
+        for v in range(2):
+            summed = held.tile([D, N], BF16, name=f"summed{v}")
+            nc.vector.tensor_tensor(summed[:], neighbours[v][:], items[v][:], ADD)
+            product = psum.tile([D, N], F32, name=f"product{v}")
             nc.tensor.matmul(product[:], weights[:], summed[:], start=True, stop=True)
-            nc.scalar.activation(half_views[v][:, lo:hi], product[:], RELU, bias=half_bias[:], scale=0.5)
+            half_view = held.tile([D, N], F32, name=f"half_view{v}")
+            nc.scalar.activation(half_view[:], product[:], RELU, bias=half_bias[:], scale=0.5)
+            half_views.append(half_view)
 
         nc.vector.tensor_tensor(store[:].indirect(offsets[:]), half_views[0][:], half_views[1][:], ADD)
-        nc.sync.dma_start(out, store[:])
+        nc.sync.dma_start(out[: D // 2, :], store[: D // 2, :])
+        nc.scalar.dma_start(out[D // 2 :, :], store[D // 2 :, :])

@@ -19,7 +19,7 @@ def tile_kgmodel_kernel(tc, base, h0, item0, h1, item1, w_out, b_out, offs, out)
         items = [held.tile([D, N], F32, name=f"items{v}") for v in range(2)]
         for v, (h, item) in enumerate(((h0, item0), (h1, item1))):
             nc.sync.dma_start(neighbours[v][:], h)
-            nc.scalar.dma_start(items[v][:], item)
+            nc.sync.dma_start(items[v][:], item)
 
         offsets = held.tile([D, N // 16], U16, name="offsets")
         nc.sync.dma_start(offsets[:], offs)
@@ -40,5 +40,4 @@ def tile_kgmodel_kernel(tc, base, h0, item0, h1, item1, w_out, b_out, offs, out)
             half_views.append(half_view)
 
         nc.vector.tensor_tensor(store[:].indirect(offsets[:]), half_views[0][:], half_views[1][:], ADD)
-        nc.sync.dma_start(out[: D // 2, :], store[: D // 2, :])
-        nc.scalar.dma_start(out[D // 2 :, :], store[D // 2 :, :])
+        nc.sync.dma_start(out, store[:])

@@ -11,15 +11,15 @@ FLOPS = 2 * 2 * D * D * N
 def tile_kgmodel_kernel(tc, base, h0, item0, h1, item1, w_out, b_out, offs, out):
     nc = tc.nc
     with tc.tile_pool(name="held", bufs=1) as held, tc.psum_pool(name="psum", bufs=1) as psum:
-        weights = held.tile([D, D], BF16, name="weights")
-        nc.sync.dma_start(weights[:], w_out)
-        bias = held.tile([D, 1], F32, name="bias")
-        nc.scalar.dma_start(bias[:], b_out)
         neighbours = [held.tile([D, N], F32, name=f"neighbours{v}") for v in range(2)]
         items = [held.tile([D, N], F32, name=f"items{v}") for v in range(2)]
         for v, (h, item) in enumerate(((h0, item0), (h1, item1))):
             nc.sync.dma_start(neighbours[v][:], h)
-            nc.sync.dma_start(items[v][:], item)
+            nc.scalar.dma_start(items[v][:], item)
+        weights = held.tile([D, D], BF16, name="weights")
+        nc.sync.dma_start(weights[:], w_out)
+        bias = held.tile([D, 1], F32, name="bias")
+        nc.scalar.dma_start(bias[:], b_out)
 
         offsets = held.tile([D, N // 16], U16, name="offsets")
         nc.sync.dma_start(offsets[:], offs)

@@ -5,6 +5,7 @@ ADD = mybir.AluOpType.add
 RELU = mybir.ActivationFunctionType.Relu
 
 D, S, N = 128, 512, 256
+PIECES = (1, 2)
 FLOPS = 2 * 2 * D * D * N
 
 
@@ -32,11 +33,14 @@ def tile_kgmodel_kernel(tc, base, h0, item0, h1, item1, w_out, b_out, offs, out)
         half_views = []
         for v in range(2):
             summed = held.tile([D, N], BF16, name=f"summed{v}")
-            nc.vector.tensor_tensor(summed[:], neighbours[v][:], items[v][:], ADD)
-            product = psum.tile([D, N], F32, name=f"product{v}")
-            nc.tensor.matmul(product[:], weights[:], summed[:], start=True, stop=True)
             half_view = held.tile([D, N], F32, name=f"half_view{v}")
-            nc.scalar.activation(half_view[:], product[:], RELU, bias=half_bias[:], scale=0.5)
+            width = N // PIECES[v]
+            for piece in range(PIECES[v]):
+                columns = slice(piece * width, (piece + 1) * width)
+                nc.vector.tensor_tensor(summed[:, columns], neighbours[v][:, columns], items[v][:, columns], ADD)
+                product = psum.tile([D, width], F32, name=f"product{v}_{piece}")
+                nc.tensor.matmul(product[:], weights[:], summed[:, columns], start=True, stop=True)
+                nc.scalar.activation(half_view[:, columns], product[:], RELU, bias=half_bias[:], scale=0.5)
             half_views.append(half_view)
 
         nc.vector.tensor_tensor(store[:].indirect(offsets[:]), half_views[0][:], half_views[1][:], ADD)

@@ -5,7 +5,7 @@ ADD = mybir.AluOpType.add
 RELU = mybir.ActivationFunctionType.Relu
 
 D, S, N = 128, 512, 256
-PIECES = (1, 2)
+PIECES = (2, 2)
 FLOPS = 2 * 2 * D * D * N
 
 

@@ -5,7 +5,7 @@ ADD = mybir.AluOpType.add
 RELU = mybir.ActivationFunctionType.Relu
 
 D, S, N = 128, 512, 256
-PIECES = (2, 2)
+PIECES = (2, 4)
 FLOPS = 2 * 2 * D * D * N
 
 
@@ -14,11 +14,12 @@ def tile_kgmodel_kernel(tc, base, h0, item0, h1, item1, w_out, b_out, offs, out)
     with tc.tile_pool(name="held", bufs=1) as held, tc.psum_pool(name="psum", bufs=1) as psum:
         neighbours = [held.tile([D, N], F32, name=f"neighbours{v}") for v in range(2)]
         items = [held.tile([D, N], F32, name=f"items{v}") for v in range(2)]
+        weights = held.tile([D, D], BF16, name="weights")
         for v, (h, item) in enumerate(((h0, item0), (h1, item1))):
             nc.sync.dma_start(neighbours[v][:], h)
             nc.scalar.dma_start(items[v][:], item)
-        weights = held.tile([D, D], BF16, name="weights")
-        nc.sync.dma_start(weights[:], w_out)
+            if v == 0:
+                nc.sync.dma_start(weights[:], w_out)
         bias = held.tile([D, 1], F32, name="bias")
         nc.scalar.dma_start(bias[:], b_out)
 

@@ -32,7 +32,11 @@ def tile_kgmodel_kernel(tc, base, h0, item0, h1, item1, w_out, b_out, offs, out)
         nc.scalar.mul(half_bias[:], bias[:], 0.5)
 
         half_views = []
+        first_item = held.tile([D, 1], F32, name="first_item")
+
         for v in range(2):
+            if v == 1:
+                nc.vector.tensor_copy(first_item[:], items[1][:, :1])
             summed = held.tile([D, N], BF16, name=f"summed{v}")
             half_view = held.tile([D, N], F32, name=f"half_view{v}")
             width = N // PIECES[v]

@@ -5,7 +5,7 @@ ADD = mybir.AluOpType.add
 RELU = mybir.ActivationFunctionType.Relu
 
 D, S, N = 128, 512, 256
-PIECES = (2, 4)
+HALF, QUARTER = N // 2, N // 4
 FLOPS = 2 * 2 * D * D * N
 
 
@@ -15,13 +15,13 @@ def tile_kgmodel_kernel(tc, base, h0, item0, h1, item1, w_out, b_out, offs, out)
         neighbours = [held.tile([D, N], F32, name=f"neighbours{v}") for v in range(2)]
         items = [held.tile([D, N], F32, name=f"items{v}") for v in range(2)]
         weights = held.tile([D, D], BF16, name="weights")
-        for v, (h, item) in enumerate(((h0, item0), (h1, item1))):
-            nc.sync.dma_start(neighbours[v][:], h)
-            nc.scalar.dma_start(items[v][:], item)
-            if v == 0:
-                nc.sync.dma_start(weights[:], w_out)
         bias = held.tile([D, 1], F32, name="bias")
-        nc.scalar.dma_start(bias[:], b_out)
+        nc.sync.dma_start(neighbours[0][:], h0)
+        nc.scalar.dma_start(items[0][:], item0)
+        nc.sync.dma_start(weights[:], w_out)
+        nc.sync.dma_start(neighbours[1][:], h1)
+        nc.scalar.dma_start(items[1][:], item1)
+        nc.sync.dma_start(bias[:], b_out)
 
         offsets = held.tile([D, N // 16], U16, name="offsets")
         nc.sync.dma_start(offsets[:], offs)
@@ -31,22 +31,23 @@ def tile_kgmodel_kernel(tc, base, h0, item0, h1, item1, w_out, b_out, offs, out)
         half_bias = held.tile([D, 1], F32, name="half_bias")
         nc.scalar.mul(half_bias[:], bias[:], 0.5)
 
-        half_views = []
+        summed = [held.tile([D, N], BF16, name=f"summed{v}") for v in range(2)]
+        half_views = [held.tile([D, N], F32, name=f"half_view{v}") for v in range(2)]
         first_item = held.tile([D, 1], F32, name="first_item")
+        product0 = psum.tile([D, N], F32, name="product0")
+        for begin in range(0, N, HALF):
+            columns = slice(begin, begin + HALF)
+            nc.vector.tensor_tensor(summed[0][:, columns], neighbours[0][:, columns], items[0][:, columns], ADD)
+            nc.tensor.matmul(product0[:, columns], weights[:], summed[0][:, columns], start=True, stop=True)
+        nc.scalar.activation(half_views[0][:], product0[:], RELU, bias=half_bias[:], scale=0.5)
 
-        for v in range(2):
-            if v == 1:
-                nc.vector.tensor_copy(first_item[:], items[1][:, :1])
-            summed = held.tile([D, N], BF16, name=f"summed{v}")
-            half_view = held.tile([D, N], F32, name=f"half_view{v}")
-            width = N // PIECES[v]
-            for piece in range(PIECES[v]):
-                columns = slice(piece * width, (piece + 1) * width)
-                nc.vector.tensor_tensor(summed[:, columns], neighbours[v][:, columns], items[v][:, columns], ADD)
-                product = psum.tile([D, width], F32, name=f"product{v}_{piece}")
-                nc.tensor.matmul(product[:], weights[:], summed[:, columns], start=True, stop=True)
-                nc.scalar.activation(half_view[:, columns], product[:], RELU, bias=half_bias[:], scale=0.5)
-            half_views.append(half_view)
+        nc.vector.tensor_copy(first_item[:], items[1][:, :1])
+        for begin in range(0, N, QUARTER):
+            columns = slice(begin, begin + QUARTER)
+            nc.vector.tensor_tensor(summed[1][:, columns], neighbours[1][:, columns], items[1][:, columns], ADD)
+            product1 = psum.tile([D, QUARTER], F32, name=f"product1_{begin}")
+            nc.tensor.matmul(product1[:], weights[:], summed[1][:, columns], start=True, stop=True)
+            nc.scalar.activation(half_views[1][:, columns], product1[:], RELU, bias=half_bias[:], scale=0.5)
 
         nc.vector.tensor_tensor(store[:].indirect(offsets[:]), half_views[0][:], half_views[1][:], ADD)
         nc.sync.dma_start(out, store[:])

@@ -33,13 +33,18 @@ def tile_kgmodel_kernel(tc, base, h0, item0, h1, item1, w_out, b_out, offs, out)
 
         summed = [held.tile([D, N], BF16, name=f"summed{v}") for v in range(2)]
         half_views = [held.tile([D, N], F32, name=f"half_view{v}") for v in range(2)]
-        first_item = held.tile([D, 1], F32, name="first_item")
-        product0 = psum.tile([D, N], F32, name="product0")
+        products0 = []
         for begin in range(0, N, HALF):
             columns = slice(begin, begin + HALF)
             nc.vector.tensor_tensor(summed[0][:, columns], neighbours[0][:, columns], items[0][:, columns], ADD)
-            nc.tensor.matmul(product0[:, columns], weights[:], summed[0][:, columns], start=True, stop=True)
-        nc.scalar.activation(half_views[0][:], product0[:], RELU, bias=half_bias[:], scale=0.5)
+            product0 = psum.tile([D, HALF], F32, name=f"product0_{begin}")
+            nc.tensor.matmul(product0[:], weights[:], summed[0][:, columns], start=True, stop=True)
+            products0.append(product0)
+        first_half = held.tile([D, HALF], F32, name="first_half")
+        nc.scalar.activation(first_half[:], products0[0][:], RELU, bias=bias[:])
+        nc.scalar.activation(half_views[0][:, HALF:], products0[1][:], RELU, bias=half_bias[:], scale=0.5)
+
+        first_item = held.tile([D, 1], F32, name="first_item")
 
         nc.vector.tensor_copy(first_item[:], items[1][:, :1])
         for begin in range(0, N, QUARTER):
@@ -48,6 +53,10 @@ def tile_kgmodel_kernel(tc, base, h0, item0, h1, item1, w_out, b_out, offs, out)
             product1 = psum.tile([D, QUARTER], F32, name=f"product1_{begin}")
             nc.tensor.matmul(product1[:], weights[:], summed[1][:, columns], start=True, stop=True)
             nc.scalar.activation(half_views[1][:, columns], product1[:], RELU, bias=half_bias[:], scale=0.5)
+
+        nc.vector.tensor_scalar_mul(half_views[0][:, :HALF], first_half[:], 0.5)
+        first_column = held.tile([D, 1], F32, name="first_column")
+        nc.vector.tensor_copy(first_column[:], half_views[0][:, :1])
 
         nc.vector.tensor_tensor(store[:].indirect(offsets[:]), half_views[0][:], half_views[1][:], ADD)
         nc.sync.dma_start(out, store[:])

import concourse.mybir as mybir

F32, BF16, U16 = mybir.dt.float32, mybir.dt.bfloat16, mybir.dt.uint16
ADD = mybir.AluOpType.add
RELU = mybir.ActivationFunctionType.Relu

D, S, N = 128, 512, 256
HALF, QUARTER = N // 2, N // 4
FLOPS = 2 * 2 * D * D * N


def tile_kgmodel_kernel(tc, base, h0, item0, h1, item1, w_out, b_out, offs, out):
    nc = tc.nc
    with tc.tile_pool(name="held", bufs=1) as held, tc.psum_pool(name="psum", bufs=1) as psum:
        neighbours = [held.tile([D, N], F32, name=f"neighbours{v}") for v in range(2)]
        items = [held.tile([D, N], F32, name=f"items{v}") for v in range(2)]
        weights = held.tile([D, D], BF16, name="weights")
        bias = held.tile([D, 1], F32, name="bias")
        nc.sync.dma_start(neighbours[0][:], h0)
        nc.scalar.dma_start(items[0][:], item0)
        nc.sync.dma_start(weights[:], w_out)
        nc.sync.dma_start(neighbours[1][:], h1)
        nc.scalar.dma_start(items[1][:], item1)
        nc.sync.dma_start(bias[:], b_out)

        offsets = held.tile([D, N // 16], U16, name="offsets")
        nc.sync.dma_start(offsets[:], offs)
        store = held.tile([D, S], F32, name="store")
        nc.gpsimd.dma_start(store[:], base)

        half_bias = held.tile([D, 1], F32, name="half_bias")
        nc.scalar.mul(half_bias[:], bias[:], 0.5)

        summed = [held.tile([D, N], BF16, name=f"summed{v}") for v in range(2)]
        half_views = [held.tile([D, N], F32, name=f"half_view{v}") for v in range(2)]
        products0 = []
        for begin in range(0, N, HALF):
            columns = slice(begin, begin + HALF)
            nc.vector.tensor_tensor(summed[0][:, columns], neighbours[0][:, columns], items[0][:, columns], ADD)
            product0 = psum.tile([D, HALF], F32, name=f"product0_{begin}")
            nc.tensor.matmul(product0[:], weights[:], summed[0][:, columns], start=True, stop=True)
            products0.append(product0)
        first_half = held.tile([D, HALF], F32, name="first_half")
        nc.scalar.activation(first_half[:], products0[0][:], RELU, bias=bias[:])
        nc.scalar.activation(half_views[0][:, HALF:], products0[1][:], RELU, bias=half_bias[:], scale=0.5)

        first_item = held.tile([D, 1], F32, name="first_item")

        nc.vector.tensor_copy(first_item[:], items[1][:, :1])
        for begin in range(0, N, QUARTER):
            columns = slice(begin, begin + QUARTER)
            nc.vector.tensor_tensor(summed[1][:, columns], neighbours[1][:, columns], items[1][:, columns], ADD)
            product1 = psum.tile([D, QUARTER], F32, name=f"product1_{begin}")
            nc.tensor.matmul(product1[:], weights[:], summed[1][:, columns], start=True, stop=True)
            nc.scalar.activation(half_views[1][:, columns], product1[:], RELU, bias=half_bias[:], scale=0.5)

        nc.vector.tensor_scalar_mul(half_views[0][:, :HALF], first_half[:], 0.5)
        first_column = held.tile([D, 1], F32, name="first_column")
        nc.vector.tensor_copy(first_column[:], half_views[0][:, :1])

        nc.vector.tensor_tensor(store[:].indirect(offsets[:]), half_views[0][:], half_views[1][:], ADD)
        nc.sync.dma_start(out, store[:])
